import numpy as np
import ml_dtypes


def mxq(x, axis, fmt="e4m3"):
    dtype, down = {"e4m3": (ml_dtypes.float8_e4m3fn, 7), "e5m2": (ml_dtypes.float8_e5m2, 14)}[fmt]
    v = np.moveaxis(np.asarray(x, np.float32).astype(ml_dtypes.bfloat16).astype(np.float64), axis, -1)
    blocks = v.reshape(v.shape[:-1] + (-1, 32))
    amax = np.abs(blocks).max(-1, keepdims=True)
    byte = np.maximum(np.where(amax > 0, np.frexp(amax)[1] - 1 + 127, 0) - down, 1)
    scale = np.exp2(byte - 127.0)
    codes = (blocks / scale).astype(np.float32).astype(dtype).astype(np.float64)
    return np.moveaxis((codes * scale).reshape(v.shape), -1, axis)


WIDE = False


def mx_kscale(k):
    if not WIDE:
        return np.ones(k)
    levels = np.array([10, -10, 5, -5, 0])
    a = np.random.permutation(np.resize(levels, k // 512 * 4)).reshape(k // 512, 4)
    idx = np.arange(k)
    return np.exp2(a[idx // 512, idx % 128 // 32])


BF16 = ml_dtypes.bfloat16


def bf(x):
    return np.asarray(x, np.float32).astype(BF16)


def f64(x):
    return np.asarray(x).astype(np.float64)


B, IN, MEM, CTX, H, G = 512, 1024, 1024, 1024, 4, 3


def sigmoid(v):
    return 1.0 / (1.0 + np.exp(-v))


def setup_inputs():
    s = mx_kscale(IN)
    w = np.random.standard_normal((MEM, MEM + IN)) / np.sqrt(MEM + IN)
    w[:, MEM:] = w[:, MEM:] / s
    return {"input_tensor": bf(np.random.standard_normal((B, IN)) * s),
            "previous_memory": bf(np.random.standard_normal((B, MEM))),
            "fg_w": bf(w),
            "fg_b": bf(np.random.standard_normal(MEM) * 0.3)}


def reference(input_tensor, previous_memory, fg_w, fg_b):
    m = f64(previous_memory)
    forget_in = np.concatenate([m, f64(input_tensor)], axis=-1)
    fgate = sigmoid((mxq(forget_in, 1, "e4m3") @ mxq(f64(fg_w), 1, "e4m3").T) + f64(fg_b))
    return m * fgate

@@ -1,0 +1,229 @@
+from contextlib import ExitStack
+
+import concourse.mybir as mybir
+from concourse.masks import make_identity
+
+F32 = mybir.dt.float32
+BF16 = mybir.dt.bfloat16
+U32 = mybir.dt.uint32
+U8 = mybir.dt.uint8
+FP8X4 = mybir.dt.float8_e4m3fn_x4
+ADD = mybir.AluOpType.add
+MULT = mybir.AluOpType.mult
+SIGMOID = mybir.ActivationFunctionType.Sigmoid
+
+P = 128
+B, IN, MEM = 512, 1024, 1024
+K = MEM + IN
+FLOPS = 2 * B * MEM * K
+
+NI = B // P
+NQ = 4
+NG = 4
+
+MANUAL = True
+TP_BUFS = 5
+ACC_BUFS = 3
+W_COPY_ON_VECTOR = ((0, 1), (0, 3))
+MULT_ON_GPSIMD = ()
+
+
+def tile_dynamicmemorycell_pa_kernel(tc, input_tensor, previous_memory, fg_w, fg_b, out):
+    nc = tc.nc
+    with ExitStack() as ctx:
+        const = ctx.enter_context(tc.tile_pool(name="const", bufs=1))
+        keep = ctx.enter_context(tc.tile_pool(name="keep", bufs=1))
+        grp_pool = ctx.enter_context(tc.tile_pool(name="grpp", bufs=4))
+        ep = ctx.enter_context(tc.tile_pool(name="ep", bufs=3))
+        tp_pool = ctx.enter_context(tc.psum_pool(name="tpp", bufs=TP_BUFS))
+        acc_pool = ctx.enter_context(tc.psum_pool(name="accp", bufs=ACC_BUFS))
+        if MANUAL:
+            ctx.enter_context(tc.manual_schedule())
+
+        brow = const.tile([P, MEM], BF16, name="brow")
+        nc.vector.memset(brow[:], 0.0)
+        nc.scalar.dma_start(out=brow[0:1, :], in_=fg_b.unsqueeze(0))
+        ones = const.tile([P, P], BF16, name="ones")
+        nc.vector.memset(ones[:], 1.0)
+        warm = const.tile([P, 1], F32, name="warm")
+        nc.vector.memset(warm[:], 0.0)
+        warm2 = const.tile([P, 1], F32, name="warm2")
+        nc.scalar.activation(out=warm2[:], in_=warm[:], func=SIGMOID)
+        ident = const.tile([P, P], F32, name="ident")
+        make_identity(nc, ident[:])
+        bias_bc = const.tile([P, MEM], F32, name="bias_bc")
+
+        x_dram = (previous_memory, input_tensor)
+        xv = [a.rearrange("(p i) k -> p i k", i=NI) for a in x_dram]
+        x_sb = [keep.tile([P, NI, 1024], BF16, name="x_sb%d" % s) for s in range(2)]
+        wv = fg_w.rearrange("(q p r) k -> q p r k", q=NQ, r=2)
+        w_sb = [keep.tile([P, 2, K], BF16, name="w_sb%d" % q) for q in range(NQ)]
+        ov = out.rearrange("(p i) n -> p i n", i=NI)
+
+        for s, lo, hi in ((0, 0, 1), (0, 1, 2), (0, 2, 4), (1, 0, 2), (1, 2, 4)):
+            nc.sync.dma_start(out=x_sb[s][:, lo:hi, :], in_=xv[s][:, lo:hi, :])
+        for h in range(2):
+            nc.sync.dma_start(
+                out=w_sb[0][:, :, 1024 * h : 1024 * (h + 1)], in_=wv[0][:, :, 1024 * h : 1024 * (h + 1)]
+            )
+        for q in range(1, NQ):
+            nc.sync.dma_start(out=w_sb[q][:], in_=wv[q])
+
+        xq = [[keep.tile([P, 256], U32, name="xq%d_%d" % (s, i), align_bytes=64) for i in range(NI)] for s in range(2)]
+        xs = [[keep.tile([P, 256], U8, name="xs%d_%d" % (s, i), align_bytes=64) for i in range(NI)] for s in range(2)]
+        wq = [[keep.tile([P, 256], U32, name="wq%d_%d" % (q, g), align_bytes=64) for g in range(NG)] for q in range(NQ)]
+        ws = [[keep.tile([P, 256], U8, name="ws%d_%d" % (q, g), align_bytes=64) for g in range(NG)] for q in range(NQ)]
+
+        def transposes(srcs):
+            tp = tp_pool.tile([P, 4, P], F32, name="tp")
+            for a in range(4):
+                nc.tensor.transpose(tp[:, a, :], srcs[a], ident[:])
+            return tp
+
+        def copy_out(engine_is_vector, dst, src):
+            if engine_is_vector:
+                nc.vector.tensor_copy(out=dst, in_=src)
+            else:
+                nc.scalar.copy(out=dst, in_=src)
+
+        def t_x(s, i):
+            words = x_sb[s][:, i, :].bitcast(F32)
+            return transposes([words[:, P * a : P * (a + 1)] for a in range(4)])
+
+        def c_x(tp, on_vector):
+            grp = grp_pool.tile([P, 1024], BF16, name="grp", align_bytes=64)
+            copy_out(
+                on_vector,
+                grp[:].bitcast(F32).rearrange("p (g c u) -> p g c u", g=2, c=P, u=2),
+                tp[:].rearrange("p (g u) c -> p g c u", g=2, u=2),
+            )
+            return grp
+
+        def t_w(q, g):
+            srcs = []
+            for r in range(2):
+                words = w_sb[q][:, r, :].bitcast(F32)
+                for u in range(2):
+                    srcs.append(words[:, 256 * g + P * u : 256 * g + P * (u + 1)])
+            return transposes(srcs)
+
+        def c_w(tp, on_vector):
+            grp = grp_pool.tile([P, 1024], BF16, name="grp", align_bytes=64)
+            copy_out(
+                on_vector,
+                grp[:].bitcast(F32).rearrange("p (c a) -> p c a", a=4),
+                tp[:].rearrange("p a c -> p c a"),
+            )
+            return grp
+
+        def quant(grp, codes, scales):
+            nc.vector.quantize_mx(out=codes[:].bitcast(FP8X4), scales=scales[:], in_=grp[:])
+
+        def mx(q, ib):
+            acc = acc_pool.tile([P, 2, 256], F32, name="acc", tag="acc")
+            for i2 in range(2):
+                i = 2 * ib + i2
+                for g in range(NG):
+                    s, gl = divmod(g, 2)
+                    cols = slice(P * gl, P * (gl + 1))
+                    nc.tensor.matmul_mx(
+                        out=acc[:, i2, :],
+                        lhsT=xq[s][i][:, cols].bitcast(FP8X4),
+                        lhsT_scale=xs[s][i][:, cols],
+                        rhs=wq[q][g][:].bitcast(FP8X4),
+                        rhs_scale=ws[q][g][:],
+                        start=(g == 0),
+                        stop=(g == NG - 1),
+                    )
+            return acc
+
+        def e1(q, acc):
+            z = ep.tile([P, 2, 256], F32, name="z")
+            nc.vector.tensor_tensor(
+                out=z[:],
+                in0=acc[:],
+                in1=bias_bc[:, 256 * q : 256 * (q + 1)].unsqueeze(1).to_broadcast([P, 2, 256]),
+                op=ADD,
+            )
+            return z
+
+        def e2(z):
+            sg = ep.tile([P, 2, 256], F32, name="sg")
+            nc.scalar.activation(out=sg[:], in_=z[:], func=SIGMOID)
+            return sg
+
+        def e3(q, ib, sg):
+            o = ep.tile([P, 2, 256], F32, name="o")
+            eng = nc.gpsimd if (q, ib) in MULT_ON_GPSIMD else nc.vector
+            eng.tensor_tensor(
+                out=o[:], in0=sg[:], in1=x_sb[0][:, 2 * ib : 2 * ib + 2, 256 * q : 256 * (q + 1)], op=MULT
+            )
+            nc.sync.dma_start(out=ov[:, 2 * ib : 2 * ib + 2, 256 * q : 256 * (q + 1)], in_=o[:])
+
+        x_units = [(s, i) for s in range(2) for i in range(NI)]
+        x_grp = {}
+        for n, (s, i) in enumerate(x_units):
+            tp = t_x(s, i)
+            x_grp[n] = c_x(tp, n % 2 == 1)
+            if n >= 1:
+                sp, ip = x_units[n - 1]
+                quant(x_grp[n - 1], xq[sp][ip], xs[sp][ip])
+            if n == 3:
+                for h in range(2):
+                    bp = acc_pool.tile([P, 512], F32, name="bp", tag="acc")
+                    nc.tensor.matmul(out=bp[:], lhsT=ones[:], rhs=brow[:, 512 * h : 512 * (h + 1)], start=True, stop=True)
+                    nc.vector.tensor_copy(out=bias_bc[:, 512 * h : 512 * (h + 1)], in_=bp[:])
+
+        w_grp = {}
+        for g in range(NG):
+            tp = t_w(0, g)
+            w_grp[(0, g)] = c_w(tp, (0, g) in W_COPY_ON_VECTOR)
+            if g == 0:
+                quant(x_grp[7], xq[1][3], xs[1][3])
+            else:
+                quant(w_grp[(0, g - 1)], wq[0][g - 1], ws[0][g - 1])
+        quant(w_grp[(0, 3)], wq[0][3], ws[0][3])
+
+        accs = {}
+        zs = {}
+        sgs = {}
+        for q in range(NQ):
+            nxt = q + 1 < NQ
+            prev = q >= 1
+            tps = [t_w(q + 1, g) for g in range(NG)] if nxt else []
+
+            def cw(g):
+                w_grp[(q + 1, g)] = c_w(tps[g], (q + 1, g) in W_COPY_ON_VECTOR)
+
+            def qw(g):
+                quant(w_grp[(q + 1, g)], wq[q + 1][g], ws[q + 1][g])
+
+            if prev:
+                zs[(q - 1, 1)] = e1(q - 1, accs[(q - 1, 1)])
+            if nxt:
+                cw(0)
+            if prev:
+                e3(q - 1, 0, sgs[(q - 1, 0)])
+                sgs[(q - 1, 1)] = e2(zs[(q - 1, 1)])
+            if nxt:
+                qw(0)
+                cw(1)
+            if prev:
+                e3(q - 1, 1, sgs[(q - 1, 1)])
+            if nxt:
+                qw(1)
+            accs[(q, 0)] = mx(q, 0)
+            if nxt:
+                cw(2)
+                cw(3)
+            zs[(q, 0)] = e1(q, accs[(q, 0)])
+            if nxt:
+                qw(2)
+                qw(3)
+            sgs[(q, 0)] = e2(zs[(q, 0)])
+            accs[(q, 1)] = mx(q, 1)
+
+        zs[(3, 1)] = e1(3, accs[(3, 1)])
+        e3(3, 0, sgs[(3, 0)])
+        sgs[(3, 1)] = e2(zs[(3, 1)])
+        e3(3, 1, sgs[(3, 1)])

@@ -16,16 +16,35 @@ P = 128
 B, IN, MEM = 512, 1024, 1024
 K = MEM + IN
 FLOPS = 2 * B * MEM * K
-
-NI = B // P
+NI = 4
 NQ = 4
 NG = 4
-
-MANUAL = True
 TP_BUFS = 5
 ACC_BUFS = 3
-W_COPY_ON_VECTOR = ((0, 1), (0, 3))
-MULT_ON_GPSIMD = ()
+SPLIT_BANKS = ((3, 1),)
+
+PROG = (
+    ("LX", 0, 0, 1), ("LX", 1, 0, 1), ("LW", 0, 0, 1024), ("LW", 0, 1024, 2048), ("LX", 0, 1, 2), ("LX", 1, 1, 2),
+    ("LW", 1, 0, 1024), ("LW", 1, 1024, 2048), ("LX", 0, 2, 4), ("LX", 1, 2, 4), ("LW", 2, 0, 2048),
+    ("LW", 3, 0, 2048), ("TX", 0, 0), ("TX", 1, 0), ("CX", 0, 0, "S"), ("CX", 1, 0, "S"), ("QX", 0, 0), ("B",),
+    ("TW", 0, 0), ("TW", 0, 1), ("TW", 0, 2), ("TW", 0, 3), ("CW", 0, 0, "S"), ("QX", 1, 0), ("CW", 0, 1, "S"),
+    ("QW", 0, 0), ("CW", 0, 2, "V"), ("QW", 0, 1), ("CW", 0, 3, "S"), ("QW", 0, 2), ("TX", 0, 1), ("TX", 1, 1),
+    ("CX", 0, 1, "S"), ("QW", 0, 3), ("CX", 1, 1, "S"), ("QX", 0, 1), ("QX", 1, 1), ("M", 0, 0), ("TW", 1, 0),
+    ("TW", 1, 1), ("TW", 1, 2), ("TW", 1, 3), ("CW", 1, 0, "S"), ("CW", 1, 1, "S"), ("QW", 1, 0), ("CW", 1, 2, "S"),
+    ("QW", 1, 1), ("CW", 1, 3, "S"), ("QW", 1, 2), ("QW", 1, 3), ("M", 0, 1), ("TX", 0, 2), ("TX", 0, 3),
+    ("TX", 1, 2), ("TX", 1, 3), ("E1", 0, 0, -1), ("CX", 0, 2, "S"), ("CX", 0, 3, "S"), ("QX", 0, 2),
+    ("CX", 1, 2, "S"), ("QX", 0, 3), ("CX", 1, 3, "S"), ("QX", 1, 2), ("E2", 0, 0, -1), ("QX", 1, 3), ("M", 1, 0),
+    ("M", 1, 1), ("TW", 2, 0), ("TW", 2, 1), ("TW", 2, 2), ("TW", 2, 3), ("E1", 1, 0, -1), ("CW", 2, 0, "S"),
+    ("E3", 0, 0, -1, "V"), ("CW", 2, 1, "S"), ("QW", 2, 0), ("CW", 2, 2, "S"), ("QW", 2, 1), ("CW", 2, 3, "S"),
+    ("QW", 2, 2), ("E2", 1, 0, -1), ("QW", 2, 3), ("M", 0, 2), ("M", 0, 3), ("M", 1, 2), ("M", 1, 3), ("TW", 3, 0),
+    ("TW", 3, 1), ("TW", 3, 2), ("TW", 3, 3), ("E1", 0, 1, -1), ("E1", 1, 1, -1), ("CW", 3, 0, "S"),
+    ("E3", 1, 0, -1, "V"), ("CW", 3, 1, "S"), ("QW", 3, 0), ("CW", 3, 2, "S"), ("QW", 3, 1), ("CW", 3, 3, "S"),
+    ("QW", 3, 2), ("E2", 0, 1, -1), ("E2", 1, 1, -1), ("QW", 3, 3), ("M", 2, 0), ("M", 2, 1), ("M", 2, 2),
+    ("M", 2, 3), ("E1", 2, 0, -1), ("E3", 0, 1, -1, "G"), ("E2", 2, 0, -1), ("E1", 2, 1, -1), ("E3", 1, 1, -1, "V"),
+    ("E2", 2, 1, -1), ("M", 3, 0), ("M", 3, 1), ("M", 3, 2), ("M", 3, 3), ("E3", 2, 0, -1, "G"), ("E1", 3, 0, -1),
+    ("E2", 3, 0, -1), ("E3", 2, 1, -1, "V"), ("E1", 3, 1, 0), ("E2", 3, 1, 0), ("E1", 3, 1, 1),
+    ("E3", 3, 0, -1, "V"), ("E2", 3, 1, 1), ("E3", 3, 1, 0, "V"), ("E3", 3, 1, 1, "V"),
+)
 
 
 def tile_dynamicmemorycell_pa_kernel(tc, input_tensor, previous_memory, fg_w, fg_b, out):
@@ -34,11 +53,10 @@ def tile_dynamicmemorycell_pa_kernel(tc, input_tensor, previous_memory, fg_w, fg
         const = ctx.enter_context(tc.tile_pool(name="const", bufs=1))
         keep = ctx.enter_context(tc.tile_pool(name="keep", bufs=1))
         grp_pool = ctx.enter_context(tc.tile_pool(name="grpp", bufs=4))
-        ep = ctx.enter_context(tc.tile_pool(name="ep", bufs=3))
+        ep = ctx.enter_context(tc.tile_pool(name="ep", bufs=5))
         tp_pool = ctx.enter_context(tc.psum_pool(name="tpp", bufs=TP_BUFS))
         acc_pool = ctx.enter_context(tc.psum_pool(name="accp", bufs=ACC_BUFS))
-        if MANUAL:
-            ctx.enter_context(tc.manual_schedule())
+        ctx.enter_context(tc.manual_schedule())
 
         brow = const.tile([P, MEM], BF16, name="brow")
         nc.vector.memset(brow[:], 0.0)
@@ -60,19 +78,16 @@ def tile_dynamicmemorycell_pa_kernel(tc, input_tensor, previous_memory, fg_w, fg
         w_sb = [keep.tile([P, 2, K], BF16, name="w_sb%d" % q) for q in range(NQ)]
         ov = out.rearrange("(p i) n -> p i n", i=NI)
 
-        for s, lo, hi in ((0, 0, 1), (0, 1, 2), (0, 2, 4), (1, 0, 2), (1, 2, 4)):
-            nc.sync.dma_start(out=x_sb[s][:, lo:hi, :], in_=xv[s][:, lo:hi, :])
-        for h in range(2):
-            nc.sync.dma_start(
-                out=w_sb[0][:, :, 1024 * h : 1024 * (h + 1)], in_=wv[0][:, :, 1024 * h : 1024 * (h + 1)]
-            )
-        for q in range(1, NQ):
-            nc.sync.dma_start(out=w_sb[q][:], in_=wv[q])
-
         xq = [[keep.tile([P, 256], U32, name="xq%d_%d" % (s, i), align_bytes=64) for i in range(NI)] for s in range(2)]
         xs = [[keep.tile([P, 256], U8, name="xs%d_%d" % (s, i), align_bytes=64) for i in range(NI)] for s in range(2)]
         wq = [[keep.tile([P, 256], U32, name="wq%d_%d" % (q, g), align_bytes=64) for g in range(NG)] for q in range(NQ)]
         ws = [[keep.tile([P, 256], U8, name="ws%d_%d" % (q, g), align_bytes=64) for g in range(NG)] for q in range(NQ)]
+
+        tps = {}
+        grps = {}
+        accs = {}
+        zs = {}
+        sgs = {}
 
         def transposes(srcs):
             tp = tp_pool.tile([P, 4, P], F32, name="tp")
@@ -80,54 +95,78 @@ def tile_dynamicmemorycell_pa_kernel(tc, input_tensor, previous_memory, fg_w, fg
                 nc.tensor.transpose(tp[:, a, :], srcs[a], ident[:])
             return tp
 
-        def copy_out(engine_is_vector, dst, src):
-            if engine_is_vector:
+        def copy_out(eng, dst, src):
+            if eng == "V":
                 nc.vector.tensor_copy(out=dst, in_=src)
             else:
                 nc.scalar.copy(out=dst, in_=src)
 
-        def t_x(s, i):
-            words = x_sb[s][:, i, :].bitcast(F32)
-            return transposes([words[:, P * a : P * (a + 1)] for a in range(4)])
-
-        def c_x(tp, on_vector):
-            grp = grp_pool.tile([P, 1024], BF16, name="grp", align_bytes=64)
-            copy_out(
-                on_vector,
-                grp[:].bitcast(F32).rearrange("p (g c u) -> p g c u", g=2, c=P, u=2),
-                tp[:].rearrange("p (g u) c -> p g c u", g=2, u=2),
-            )
-            return grp
-
-        def t_w(q, g):
-            srcs = []
-            for r in range(2):
-                words = w_sb[q][:, r, :].bitcast(F32)
-                for u in range(2):
-                    srcs.append(words[:, 256 * g + P * u : 256 * g + P * (u + 1)])
-            return transposes(srcs)
-
-        def c_w(tp, on_vector):
-            grp = grp_pool.tile([P, 1024], BF16, name="grp", align_bytes=64)
-            copy_out(
-                on_vector,
-                grp[:].bitcast(F32).rearrange("p (c a) -> p c a", a=4),
-                tp[:].rearrange("p a c -> p c a"),
-            )
-            return grp
-
-        def quant(grp, codes, scales):
-            nc.vector.quantize_mx(out=codes[:].bitcast(FP8X4), scales=scales[:], in_=grp[:])
-
-        def mx(q, ib):
-            acc = acc_pool.tile([P, 2, 256], F32, name="acc", tag="acc")
-            for i2 in range(2):
-                i = 2 * ib + i2
+        for op in PROG:
+            kind = op[0]
+            if kind == "LX":
+                s, lo, hi = op[1], op[2], op[3]
+                nc.sync.dma_start(out=x_sb[s][:, lo:hi, :], in_=xv[s][:, lo:hi, :])
+            elif kind == "LW":
+                q, lo, hi = op[1], op[2], op[3]
+                nc.sync.dma_start(out=w_sb[q][:, :, lo:hi], in_=wv[q][:, :, lo:hi])
+            elif kind == "TX":
+                s, i = op[1], op[2]
+                words = x_sb[s][:, i, :].bitcast(F32)
+                tps[("X", s, i)] = transposes([words[:, P * a : P * (a + 1)] for a in range(4)])
+            elif kind == "TW":
+                q, g = op[1], op[2]
+                srcs = []
+                for r in range(2):
+                    words = w_sb[q][:, r, :].bitcast(F32)
+                    for u in range(2):
+                        srcs.append(words[:, 256 * g + P * u : 256 * g + P * (u + 1)])
+                tps[("W", q, g)] = transposes(srcs)
+            elif kind == "CX":
+                grp = grp_pool.tile([P, 1024], BF16, name="grp", align_bytes=64)
+                copy_out(
+                    op[3],
+                    grp[:].bitcast(F32).rearrange("p (g c u) -> p g c u", g=2, c=P, u=2),
+                    tps[("X", op[1], op[2])][:].rearrange("p (g u) c -> p g c u", g=2, u=2),
+                )
+                grps[("X", op[1], op[2])] = grp
+            elif kind == "CW":
+                grp = grp_pool.tile([P, 1024], BF16, name="grp", align_bytes=64)
+                copy_out(
+                    op[3],
+                    grp[:].bitcast(F32).rearrange("p (c a) -> p c a", a=4),
+                    tps[("W", op[1], op[2])][:].rearrange("p a c -> p c a"),
+                )
+                grps[("W", op[1], op[2])] = grp
+            elif kind == "QX":
+                s, i = op[1], op[2]
+                nc.vector.quantize_mx(out=xq[s][i][:].bitcast(FP8X4), scales=xs[s][i][:], in_=grps[("X", s, i)][:])
+            elif kind == "QW":
+                q, g = op[1], op[2]
+                nc.vector.quantize_mx(out=wq[q][g][:].bitcast(FP8X4), scales=ws[q][g][:], in_=grps[("W", q, g)][:])
+            elif kind == "B":
+                for h in range(2):
+                    bp = acc_pool.tile([P, 512], F32, name="bp", tag="acc")
+                    nc.tensor.matmul(
+                        out=bp[:], lhsT=ones[:], rhs=brow[:, 512 * h : 512 * (h + 1)], start=True, stop=True
+                    )
+                    copy_out("SV"[h], bias_bc[:, 512 * h : 512 * (h + 1)], bp[:])
+            elif kind == "M":
+                q, i = op[1], op[2]
+                ib, i2 = divmod(i, 2)
+                if (q, ib) in SPLIT_BANKS:
+                    acch = acc_pool.tile([P, 256], F32, name="acch", tag="acc")
+                    accs[(q, ib, i2)] = acch
+                    dst = acch[:]
+                else:
+                    if i2 == 0:
+                        acc = acc_pool.tile([P, 2, 256], F32, name="acc", tag="acc")
+                        accs[(q, ib)] = acc
+                    dst = accs[(q, ib)][:, i2, :]
                 for g in range(NG):
                     s, gl = divmod(g, 2)
                     cols = slice(P * gl, P * (gl + 1))
                     nc.tensor.matmul_mx(
-                        out=acc[:, i2, :],
+                        out=dst,
                         lhsT=xq[s][i][:, cols].bitcast(FP8X4),
                         lhsT_scale=xs[s][i][:, cols],
                         rhs=wq[q][g][:].bitcast(FP8X4),
@@ -135,95 +174,38 @@ def tile_dynamicmemorycell_pa_kernel(tc, input_tensor, previous_memory, fg_w, fg
                         start=(g == 0),
                         stop=(g == NG - 1),
                     )
-            return acc
-
-        def e1(q, acc):
-            z = ep.tile([P, 2, 256], F32, name="z")
-            nc.vector.tensor_tensor(
-                out=z[:],
-                in0=acc[:],
-                in1=bias_bc[:, 256 * q : 256 * (q + 1)].unsqueeze(1).to_broadcast([P, 2, 256]),
-                op=ADD,
-            )
-            return z
-
-        def e2(z):
-            sg = ep.tile([P, 2, 256], F32, name="sg")
-            nc.scalar.activation(out=sg[:], in_=z[:], func=SIGMOID)
-            return sg
-
-        def e3(q, ib, sg):
-            o = ep.tile([P, 2, 256], F32, name="o")
-            eng = nc.gpsimd if (q, ib) in MULT_ON_GPSIMD else nc.vector
-            eng.tensor_tensor(
-                out=o[:], in0=sg[:], in1=x_sb[0][:, 2 * ib : 2 * ib + 2, 256 * q : 256 * (q + 1)], op=MULT
-            )
-            nc.sync.dma_start(out=ov[:, 2 * ib : 2 * ib + 2, 256 * q : 256 * (q + 1)], in_=o[:])
-
-        x_units = [(s, i) for s in range(2) for i in range(NI)]
-        x_grp = {}
-        for n, (s, i) in enumerate(x_units):
-            tp = t_x(s, i)
-            x_grp[n] = c_x(tp, n % 2 == 1)
-            if n >= 1:
-                sp, ip = x_units[n - 1]
-                quant(x_grp[n - 1], xq[sp][ip], xs[sp][ip])
-            if n == 3:
-                for h in range(2):
-                    bp = acc_pool.tile([P, 512], F32, name="bp", tag="acc")
-                    nc.tensor.matmul(out=bp[:], lhsT=ones[:], rhs=brow[:, 512 * h : 512 * (h + 1)], start=True, stop=True)
-                    nc.vector.tensor_copy(out=bias_bc[:, 512 * h : 512 * (h + 1)], in_=bp[:])
-
-        w_grp = {}
-        for g in range(NG):
-            tp = t_w(0, g)
-            w_grp[(0, g)] = c_w(tp, (0, g) in W_COPY_ON_VECTOR)
-            if g == 0:
-                quant(x_grp[7], xq[1][3], xs[1][3])
-            else:
-                quant(w_grp[(0, g - 1)], wq[0][g - 1], ws[0][g - 1])
-        quant(w_grp[(0, 3)], wq[0][3], ws[0][3])
-
-        accs = {}
-        zs = {}
-        sgs = {}
-        for q in range(NQ):
-            nxt = q + 1 < NQ
-            prev = q >= 1
-            tps = [t_w(q + 1, g) for g in range(NG)] if nxt else []
-
-            def cw(g):
-                w_grp[(q + 1, g)] = c_w(tps[g], (q + 1, g) in W_COPY_ON_VECTOR)
-
-            def qw(g):
-                quant(w_grp[(q + 1, g)], wq[q + 1][g], ws[q + 1][g])
-
-            if prev:
-                zs[(q - 1, 1)] = e1(q - 1, accs[(q - 1, 1)])
-            if nxt:
-                cw(0)
-            if prev:
-                e3(q - 1, 0, sgs[(q - 1, 0)])
-                sgs[(q - 1, 1)] = e2(zs[(q - 1, 1)])
-            if nxt:
-                qw(0)
-                cw(1)
-            if prev:
-                e3(q - 1, 1, sgs[(q - 1, 1)])
-            if nxt:
-                qw(1)
-            accs[(q, 0)] = mx(q, 0)
-            if nxt:
-                cw(2)
-                cw(3)
-            zs[(q, 0)] = e1(q, accs[(q, 0)])
-            if nxt:
-                qw(2)
-                qw(3)
-            sgs[(q, 0)] = e2(zs[(q, 0)])
-            accs[(q, 1)] = mx(q, 1)
-
-        zs[(3, 1)] = e1(3, accs[(3, 1)])
-        e3(3, 0, sgs[(3, 0)])
-        sgs[(3, 1)] = e2(zs[(3, 1)])
-        e3(3, 1, sgs[(3, 1)])
+            elif kind == "E1":
+                q, ib, h = op[1], op[2], op[3]
+                bias = bias_bc[:, 256 * q : 256 * (q + 1)]
+                if h < 0:
+                    z = ep.tile([P, 2, 256], F32, name="z")
+                    nc.vector.tensor_tensor(
+                        out=z[:], in0=accs[(q, ib)][:], in1=bias.unsqueeze(1).to_broadcast([P, 2, 256]), op=ADD
+                    )
+                    zs[(q, ib, h)] = z
+                else:
+                    zh = ep.tile([P, 256], F32, name="zh")
+                    nc.vector.tensor_tensor(out=zh[:], in0=accs[(q, ib, h)][:], in1=bias, op=ADD)
+                    zs[(q, ib, h)] = zh
+            elif kind == "E2":
+                q, ib, h = op[1], op[2], op[3]
+                if h < 0:
+                    sg = ep.tile([P, 2, 256], F32, name="sg")
+                    nc.scalar.activation(out=sg[:], in_=zs[(q, ib, h)][:], func=SIGMOID)
+                    sgs[(q, ib, h)] = sg
+                else:
+                    sgh = ep.tile([P, 256], F32, name="sgh")
+                    nc.scalar.activation(out=sgh[:], in_=zs[(q, ib, h)][:], func=SIGMOID)
+                    sgs[(q, ib, h)] = sgh
+            elif kind == "E3":
+                q, ib, h = op[1], op[2], op[3]
+                eng = nc.gpsimd if op[4] == "G" else nc.vector
+                cols = slice(256 * q, 256 * (q + 1))
+                if h < 0:
+                    o = ep.tile([P, 2, 256], F32, name="o")
+                    eng.tensor_tensor(out=o[:], in0=sgs[(q, ib, h)][:], in1=x_sb[0][:, 2 * ib : 2 * ib + 2, cols], op=MULT)
+                    nc.sync.dma_start(out=ov[:, 2 * ib : 2 * ib + 2, cols], in_=o[:])
+                else:
+                    oh = ep.tile([P, 256], F32, name="oh")
+                    eng.tensor_tensor(out=oh[:], in0=sgs[(q, ib, h)][:], in1=x_sb[0][:, 2 * ib + h, cols], op=MULT)
+                    nc.sync.dma_start(out=ov[:, 2 * ib + h, cols], in_=oh[:])

@@ -26,15 +26,16 @@ SPLIT_BANKS = ((3, 1),)
 PROG = (
     ("LX", 0, 0, 1), ("LX", 1, 0, 1), ("LW", 0, 0, 1024), ("LW", 0, 1024, 2048), ("LX", 0, 1, 2), ("LX", 1, 1, 2),
     ("LW", 1, 0, 1024), ("LW", 1, 1024, 2048), ("LX", 0, 2, 4), ("LX", 1, 2, 4), ("LW", 2, 0, 2048),
-    ("LW", 3, 0, 2048), ("TX", 0, 0), ("TX", 1, 0), ("CX", 0, 0, "S"), ("CX", 1, 0, "S"), ("QX", 0, 0), ("B",),
-    ("TW", 0, 0), ("TW", 0, 1), ("TW", 0, 2), ("TW", 0, 3), ("CW", 0, 0, "S"), ("QX", 1, 0), ("CW", 0, 1, "S"),
-    ("QW", 0, 0), ("CW", 0, 2, "V"), ("QW", 0, 1), ("CW", 0, 3, "S"), ("QW", 0, 2), ("TX", 0, 1), ("TX", 1, 1),
-    ("CX", 0, 1, "S"), ("QW", 0, 3), ("CX", 1, 1, "S"), ("QX", 0, 1), ("QX", 1, 1), ("M", 0, 0), ("TW", 1, 0),
-    ("TW", 1, 1), ("TW", 1, 2), ("TW", 1, 3), ("CW", 1, 0, "S"), ("CW", 1, 1, "S"), ("QW", 1, 0), ("CW", 1, 2, "S"),
-    ("QW", 1, 1), ("CW", 1, 3, "S"), ("QW", 1, 2), ("QW", 1, 3), ("M", 0, 1), ("TX", 0, 2), ("TX", 0, 3),
-    ("TX", 1, 2), ("TX", 1, 3), ("E1", 0, 0, -1), ("CX", 0, 2, "S"), ("CX", 0, 3, "S"), ("QX", 0, 2),
-    ("CX", 1, 2, "S"), ("QX", 0, 3), ("CX", 1, 3, "S"), ("QX", 1, 2), ("E2", 0, 0, -1), ("QX", 1, 3), ("M", 1, 0),
-    ("M", 1, 1), ("TW", 2, 0), ("TW", 2, 1), ("TW", 2, 2), ("TW", 2, 3), ("E1", 1, 0, -1), ("CW", 2, 0, "S"),
+    ("LW", 3, 0, 2048), ("D",), ("D",), ("D",), ("D",), ("D",), ("D",), ("TX", 0, 0), ("TX", 1, 0),
+    ("CX", 0, 0, "S"), ("CX", 1, 0, "S"), ("QX", 0, 0), ("B",), ("TW", 0, 0), ("TW", 0, 1), ("D",), ("TW", 0, 2),
+    ("TW", 0, 3), ("D",), ("CW", 0, 0, "S"), ("QX", 1, 0), ("CW", 0, 1, "S"), ("QW", 0, 0), ("CW", 0, 2, "V"),
+    ("QW", 0, 1), ("CW", 0, 3, "S"), ("QW", 0, 2), ("TX", 0, 1), ("TX", 1, 1), ("D",), ("CX", 0, 1, "S"),
+    ("QW", 0, 3), ("CX", 1, 1, "S"), ("QX", 0, 1), ("QX", 1, 1), ("M", 0, 0), ("TW", 1, 0), ("TW", 1, 1), ("D",),
+    ("TW", 1, 2), ("TW", 1, 3), ("CW", 1, 0, "S"), ("CW", 1, 1, "S"), ("QW", 1, 0), ("CW", 1, 2, "S"), ("QW", 1, 1),
+    ("CW", 1, 3, "S"), ("QW", 1, 2), ("QW", 1, 3), ("M", 0, 1), ("TX", 0, 2), ("TX", 0, 3), ("TX", 1, 2),
+    ("TX", 1, 3), ("E1", 0, 0, -1), ("CX", 0, 2, "S"), ("CX", 0, 3, "S"), ("QX", 0, 2), ("CX", 1, 2, "S"),
+    ("QX", 0, 3), ("CX", 1, 3, "S"), ("QX", 1, 2), ("E2", 0, 0, -1), ("QX", 1, 3), ("M", 1, 0), ("M", 1, 1),
+    ("TW", 2, 0), ("TW", 2, 1), ("TW", 2, 2), ("TW", 2, 3), ("E1", 1, 0, -1), ("CW", 2, 0, "S"),
     ("E3", 0, 0, -1, "V"), ("CW", 2, 1, "S"), ("QW", 2, 0), ("CW", 2, 2, "S"), ("QW", 2, 1), ("CW", 2, 3, "S"),
     ("QW", 2, 2), ("E2", 1, 0, -1), ("QW", 2, 3), ("M", 0, 2), ("M", 0, 3), ("M", 1, 2), ("M", 1, 3), ("TW", 3, 0),
     ("TW", 3, 1), ("TW", 3, 2), ("TW", 3, 3), ("E1", 0, 1, -1), ("E1", 1, 1, -1), ("CW", 3, 0, "S"),
@@ -58,11 +59,13 @@ def tile_dynamicmemorycell_pa_kernel(tc, input_tensor, previous_memory, fg_w, fg
         acc_pool = ctx.enter_context(tc.psum_pool(name="accp", bufs=ACC_BUFS))
         ctx.enter_context(tc.manual_schedule())
 
+        ones = const.tile([P, P], BF16, name="ones")
+        nc.vector.memset(ones[:], 1.0)
+        zt = const.tile([P, 512], BF16, name="zt")
+        nc.vector.memset(zt[:], 0.0)
         brow = const.tile([P, MEM], BF16, name="brow")
         nc.vector.memset(brow[:], 0.0)
         nc.scalar.dma_start(out=brow[0:1, :], in_=fg_b.unsqueeze(0))
-        ones = const.tile([P, P], BF16, name="ones")
-        nc.vector.memset(ones[:], 1.0)
         warm = const.tile([P, 1], F32, name="warm")
         nc.vector.memset(warm[:], 0.0)
         warm2 = const.tile([P, 1], F32, name="warm2")
@@ -150,6 +153,9 @@ def tile_dynamicmemorycell_pa_kernel(tc, input_tensor, previous_memory, fg_w, fg
                         out=bp[:], lhsT=ones[:], rhs=brow[:, 512 * h : 512 * (h + 1)], start=True, stop=True
                     )
                     copy_out("SV"[h], bias_bc[:, 512 * h : 512 * (h + 1)], bp[:])
+            elif kind == "D":
+                dm = acc_pool.tile([P, 512], F32, name="dm", tag="acc")
+                nc.tensor.matmul(out=dm[:], lhsT=ones[:], rhs=zt[:], start=True, stop=True)
             elif kind == "M":
                 q, i = op[1], op[2]
                 ib, i2 = divmod(i, 2)

@@ -16,36 +16,26 @@ P = 128
 B, IN, MEM = 512, 1024, 1024
 K = MEM + IN
 FLOPS = 2 * B * MEM * K
-NI = 4
-NQ = 4
-NG = 4
-TP_BUFS = 5
-ACC_BUFS = 3
-SPLIT_BANKS = ((3, 1),)
 
-PROG = (
-    ("LX", 0, 0, 1), ("LX", 1, 0, 1), ("LW", 0, 0, 1024), ("LW", 0, 1024, 2048), ("LX", 0, 1, 2), ("LX", 1, 1, 2),
-    ("LW", 1, 0, 1024), ("LW", 1, 1024, 2048), ("LX", 0, 2, 4), ("LX", 1, 2, 4), ("LW", 2, 0, 2048),
-    ("LW", 3, 0, 2048), ("D",), ("D",), ("D",), ("D",), ("D",), ("D",), ("TX", 0, 0), ("TX", 1, 0),
-    ("CX", 0, 0, "S"), ("CX", 1, 0, "S"), ("QX", 0, 0), ("B",), ("TW", 0, 0), ("TW", 0, 1), ("D",), ("TW", 0, 2),
-    ("TW", 0, 3), ("D",), ("CW", 0, 0, "S"), ("QX", 1, 0), ("CW", 0, 1, "S"), ("QW", 0, 0), ("CW", 0, 2, "V"),
-    ("QW", 0, 1), ("CW", 0, 3, "S"), ("QW", 0, 2), ("TX", 0, 1), ("TX", 1, 1), ("D",), ("CX", 0, 1, "S"),
-    ("QW", 0, 3), ("CX", 1, 1, "S"), ("QX", 0, 1), ("QX", 1, 1), ("M", 0, 0), ("TW", 1, 0), ("TW", 1, 1), ("D",),
-    ("TW", 1, 2), ("TW", 1, 3), ("CW", 1, 0, "S"), ("CW", 1, 1, "S"), ("QW", 1, 0), ("CW", 1, 2, "S"), ("QW", 1, 1),
-    ("CW", 1, 3, "S"), ("QW", 1, 2), ("QW", 1, 3), ("M", 0, 1), ("TX", 0, 2), ("TX", 0, 3), ("TX", 1, 2),
-    ("TX", 1, 3), ("E1", 0, 0, -1), ("CX", 0, 2, "S"), ("CX", 0, 3, "S"), ("QX", 0, 2), ("CX", 1, 2, "S"),
-    ("QX", 0, 3), ("CX", 1, 3, "S"), ("QX", 1, 2), ("E2", 0, 0, -1), ("QX", 1, 3), ("M", 1, 0), ("M", 1, 1),
-    ("TW", 2, 0), ("TW", 2, 1), ("TW", 2, 2), ("TW", 2, 3), ("E1", 1, 0, -1), ("CW", 2, 0, "S"),
-    ("E3", 0, 0, -1, "V"), ("CW", 2, 1, "S"), ("QW", 2, 0), ("CW", 2, 2, "S"), ("QW", 2, 1), ("CW", 2, 3, "S"),
-    ("QW", 2, 2), ("E2", 1, 0, -1), ("QW", 2, 3), ("M", 0, 2), ("M", 0, 3), ("M", 1, 2), ("M", 1, 3), ("TW", 3, 0),
-    ("TW", 3, 1), ("TW", 3, 2), ("TW", 3, 3), ("E1", 0, 1, -1), ("E1", 1, 1, -1), ("CW", 3, 0, "S"),
-    ("E3", 1, 0, -1, "V"), ("CW", 3, 1, "S"), ("QW", 3, 0), ("CW", 3, 2, "S"), ("QW", 3, 1), ("CW", 3, 3, "S"),
-    ("QW", 3, 2), ("E2", 0, 1, -1), ("E2", 1, 1, -1), ("QW", 3, 3), ("M", 2, 0), ("M", 2, 1), ("M", 2, 2),
-    ("M", 2, 3), ("E1", 2, 0, -1), ("E3", 0, 1, -1, "G"), ("E2", 2, 0, -1), ("E1", 2, 1, -1), ("E3", 1, 1, -1, "V"),
-    ("E2", 2, 1, -1), ("M", 3, 0), ("M", 3, 1), ("M", 3, 2), ("M", 3, 3), ("E3", 2, 0, -1, "G"), ("E1", 3, 0, -1),
-    ("E2", 3, 0, -1), ("E3", 2, 1, -1, "V"), ("E1", 3, 1, 0), ("E2", 3, 1, 0), ("E1", 3, 1, 1),
-    ("E3", 3, 0, -1, "V"), ("E2", 3, 1, 1), ("E3", 3, 1, 0, "V"), ("E3", 3, 1, 1, "V"),
-)
+ROW_TILES = B // P
+GROUP = 256
+GROUPS = MEM // GROUP
+PASSES = K // (4 * P)
+WORDS = 2 * P
+PER_BANK = 4
+UNITS = 4
+
+STAGES = (("x", 0), ("w", 0), ("x", 1), ("w", 1), ("w", 2), ("w", 3))
+
+
+def output_banks(stage):
+    if stage < 0 or stage >= len(STAGES):
+        return []
+    kind, index = STAGES[stage]
+    seen = STAGES[:stage]
+    if kind == "x":
+        return [(q, index) for q in range(GROUPS) if ("w", q) in seen]
+    return [(index, h) for h in range(2) if ("x", h) in seen]
 
 
 def tile_dynamicmemorycell_pa_kernel(tc, input_tensor, previous_memory, fg_w, fg_b, out):
@@ -53,165 +43,144 @@ def tile_dynamicmemorycell_pa_kernel(tc, input_tensor, previous_memory, fg_w, fg
     with ExitStack() as ctx:
         const = ctx.enter_context(tc.tile_pool(name="const", bufs=1))
         keep = ctx.enter_context(tc.tile_pool(name="keep", bufs=1))
-        grp_pool = ctx.enter_context(tc.tile_pool(name="grpp", bufs=4))
-        ep = ctx.enter_context(tc.tile_pool(name="ep", bufs=5))
-        tp_pool = ctx.enter_context(tc.psum_pool(name="tpp", bufs=TP_BUFS))
-        acc_pool = ctx.enter_context(tc.psum_pool(name="accp", bufs=ACC_BUFS))
+        grouped_pool = ctx.enter_context(tc.tile_pool(name="grouped_pool", bufs=6))
+        gate_pool = ctx.enter_context(tc.tile_pool(name="gate_pool", bufs=4))
+        turned_pool = ctx.enter_context(tc.psum_pool(name="turned_pool", bufs=5))
+        acc_pool = ctx.enter_context(tc.psum_pool(name="acc_pool", bufs=3))
         ctx.enter_context(tc.manual_schedule())
 
+        bias_row = const.tile([P, MEM], BF16, name="bias_row")
+        nc.vector.memset(bias_row[:], 0.0)
+        nc.scalar.dma_start(out=bias_row[0:1, :], in_=fg_b.unsqueeze(0))
         ones = const.tile([P, P], BF16, name="ones")
         nc.vector.memset(ones[:], 1.0)
-        zt = const.tile([P, 512], BF16, name="zt")
-        nc.vector.memset(zt[:], 0.0)
-        brow = const.tile([P, MEM], BF16, name="brow")
-        nc.vector.memset(brow[:], 0.0)
-        nc.scalar.dma_start(out=brow[0:1, :], in_=fg_b.unsqueeze(0))
-        warm = const.tile([P, 1], F32, name="warm")
-        nc.vector.memset(warm[:], 0.0)
-        warm2 = const.tile([P, 1], F32, name="warm2")
-        nc.scalar.activation(out=warm2[:], in_=warm[:], func=SIGMOID)
+        zero_col = const.tile([P, 1], F32, name="zero_col")
+        nc.vector.memset(zero_col[:], 0.0)
+        half_col = const.tile([P, 1], F32, name="half_col")
+        nc.scalar.activation(out=half_col[:], in_=zero_col[:], func=SIGMOID)
         ident = const.tile([P, P], F32, name="ident")
         make_identity(nc, ident[:])
-        bias_bc = const.tile([P, MEM], F32, name="bias_bc")
+        bias_all = const.tile([P, MEM], F32, name="bias_all")
 
-        x_dram = (previous_memory, input_tensor)
-        xv = [a.rearrange("(p i) k -> p i k", i=NI) for a in x_dram]
-        x_sb = [keep.tile([P, NI, 1024], BF16, name="x_sb%d" % s) for s in range(2)]
-        wv = fg_w.rearrange("(q p r) k -> q p r k", q=NQ, r=2)
-        w_sb = [keep.tile([P, 2, K], BF16, name="w_sb%d" % q) for q in range(NQ)]
-        ov = out.rearrange("(p i) n -> p i n", i=NI)
+        x_dram = [a.rearrange("(p i) k -> p i k", i=ROW_TILES) for a in (previous_memory, input_tensor)]
+        x_sb = [keep.tile([P, ROW_TILES, MEM], BF16, name="x_sb%d" % s) for s in range(2)]
+        w_dram = fg_w.rearrange("(q c r) k -> q c r k", q=GROUPS, r=2)
+        w_sb = [keep.tile([P, 2, K], BF16, name="w_sb%d" % q) for q in range(GROUPS)]
+        out_dram = out.rearrange("(p i) n -> p i n", i=ROW_TILES)
+        for kind, index in STAGES:
+            for s in range(2):
+                if kind == "x":
+                    rows = slice(2 * index, 2 * index + 2)
+                    nc.sync.dma_start(out=x_sb[s][:, rows, :], in_=x_dram[s][:, rows, :])
+                else:
+                    cols = slice(MEM * s, MEM * (s + 1))
+                    nc.sync.dma_start(out=w_sb[index][:, :, cols], in_=w_dram[index][:, :, cols])
 
-        xq = [[keep.tile([P, 256], U32, name="xq%d_%d" % (s, i), align_bytes=64) for i in range(NI)] for s in range(2)]
-        xs = [[keep.tile([P, 256], U8, name="xs%d_%d" % (s, i), align_bytes=64) for i in range(NI)] for s in range(2)]
-        wq = [[keep.tile([P, 256], U32, name="wq%d_%d" % (q, g), align_bytes=64) for g in range(NG)] for q in range(NQ)]
-        ws = [[keep.tile([P, 256], U8, name="ws%d_%d" % (q, g), align_bytes=64) for g in range(NG)] for q in range(NQ)]
+        def operand_tiles(label, dtype, outer, inner):
+            return [
+                [keep.tile([P, GROUP], dtype, name="%s%d_%d" % (label, a, b), align_bytes=64) for b in range(inner)]
+                for a in range(outer)
+            ]
 
-        tps = {}
-        grps = {}
-        accs = {}
-        zs = {}
-        sgs = {}
+        x_codes, x_scales = operand_tiles("x_codes", U32, 2, ROW_TILES), operand_tiles("x_scales", U8, 2, ROW_TILES)
+        w_codes, w_scales = operand_tiles("w_codes", U32, GROUPS, PASSES), operand_tiles("w_scales", U8, GROUPS, PASSES)
 
-        def transposes(srcs):
-            tp = tp_pool.tile([P, 4, P], F32, name="tp")
-            for a in range(4):
-                nc.tensor.transpose(tp[:, a, :], srcs[a], ident[:])
-            return tp
+        def transpose_unit(stage, unit):
+            kind, index = STAGES[stage]
+            turned = turned_pool.tile([P, PER_BANK, P], F32, name="turned")
+            for a in range(PER_BANK):
+                if kind == "x":
+                    words = x_sb[unit // 2][:, 2 * index + unit % 2, :].bitcast(F32)
+                    first = P * a
+                else:
+                    words = w_sb[index][:, a // 2, :].bitcast(F32)
+                    first = WORDS * unit + P * (a % 2)
+                nc.tensor.transpose(turned[:, a, :], words[:, first : first + P], ident[:])
+            return turned
 
-        def copy_out(eng, dst, src):
-            if eng == "V":
-                nc.vector.tensor_copy(out=dst, in_=src)
+        def copy_unit(stage, turned):
+            grouped = grouped_pool.tile([P, 4 * 2 * P], BF16, name="grouped", align_bytes=64)
+            if STAGES[stage][0] == "x":
+                dst = grouped[:].bitcast(F32).rearrange("p (g c u) -> p g c u", g=2, u=2)
+                src = turned[:].rearrange("p (g u) c -> p g c u", g=2)
             else:
-                nc.scalar.copy(out=dst, in_=src)
+                dst = grouped[:].bitcast(F32).rearrange("p (c a) -> p c a", a=PER_BANK)
+                src = turned[:].rearrange("p a c -> p c a")
+            nc.scalar.copy(out=dst, in_=src)
+            return grouped
 
-        for op in PROG:
-            kind = op[0]
-            if kind == "LX":
-                s, lo, hi = op[1], op[2], op[3]
-                nc.sync.dma_start(out=x_sb[s][:, lo:hi, :], in_=xv[s][:, lo:hi, :])
-            elif kind == "LW":
-                q, lo, hi = op[1], op[2], op[3]
-                nc.sync.dma_start(out=w_sb[q][:, :, lo:hi], in_=wv[q][:, :, lo:hi])
-            elif kind == "TX":
-                s, i = op[1], op[2]
-                words = x_sb[s][:, i, :].bitcast(F32)
-                tps[("X", s, i)] = transposes([words[:, P * a : P * (a + 1)] for a in range(4)])
-            elif kind == "TW":
-                q, g = op[1], op[2]
-                srcs = []
-                for r in range(2):
-                    words = w_sb[q][:, r, :].bitcast(F32)
-                    for u in range(2):
-                        srcs.append(words[:, 256 * g + P * u : 256 * g + P * (u + 1)])
-                tps[("W", q, g)] = transposes(srcs)
-            elif kind == "CX":
-                grp = grp_pool.tile([P, 1024], BF16, name="grp", align_bytes=64)
-                copy_out(
-                    op[3],
-                    grp[:].bitcast(F32).rearrange("p (g c u) -> p g c u", g=2, c=P, u=2),
-                    tps[("X", op[1], op[2])][:].rearrange("p (g u) c -> p g c u", g=2, u=2),
-                )
-                grps[("X", op[1], op[2])] = grp
-            elif kind == "CW":
-                grp = grp_pool.tile([P, 1024], BF16, name="grp", align_bytes=64)
-                copy_out(
-                    op[3],
-                    grp[:].bitcast(F32).rearrange("p (c a) -> p c a", a=4),
-                    tps[("W", op[1], op[2])][:].rearrange("p a c -> p c a"),
-                )
-                grps[("W", op[1], op[2])] = grp
-            elif kind == "QX":
-                s, i = op[1], op[2]
-                nc.vector.quantize_mx(out=xq[s][i][:].bitcast(FP8X4), scales=xs[s][i][:], in_=grps[("X", s, i)][:])
-            elif kind == "QW":
-                q, g = op[1], op[2]
-                nc.vector.quantize_mx(out=wq[q][g][:].bitcast(FP8X4), scales=ws[q][g][:], in_=grps[("W", q, g)][:])
-            elif kind == "B":
-                for h in range(2):
-                    bp = acc_pool.tile([P, 512], F32, name="bp", tag="acc")
-                    nc.tensor.matmul(
-                        out=bp[:], lhsT=ones[:], rhs=brow[:, 512 * h : 512 * (h + 1)], start=True, stop=True
-                    )
-                    copy_out("SV"[h], bias_bc[:, 512 * h : 512 * (h + 1)], bp[:])
-            elif kind == "D":
-                dm = acc_pool.tile([P, 512], F32, name="dm", tag="acc")
-                nc.tensor.matmul(out=dm[:], lhsT=ones[:], rhs=zt[:], start=True, stop=True)
-            elif kind == "M":
-                q, i = op[1], op[2]
-                ib, i2 = divmod(i, 2)
-                if (q, ib) in SPLIT_BANKS:
-                    acch = acc_pool.tile([P, 256], F32, name="acch", tag="acc")
-                    accs[(q, ib, i2)] = acch
-                    dst = acch[:]
-                else:
-                    if i2 == 0:
-                        acc = acc_pool.tile([P, 2, 256], F32, name="acc", tag="acc")
-                        accs[(q, ib)] = acc
-                    dst = accs[(q, ib)][:, i2, :]
-                for g in range(NG):
-                    s, gl = divmod(g, 2)
-                    cols = slice(P * gl, P * (gl + 1))
+        def quantise_unit(stage, unit, grouped):
+            kind, index = STAGES[stage]
+            if kind == "x":
+                codes, scales = x_codes[unit // 2][2 * index + unit % 2], x_scales[unit // 2][2 * index + unit % 2]
+            else:
+                codes, scales = w_codes[index][unit], w_scales[index][unit]
+            nc.vector.quantize_mx(out=codes[:].bitcast(FP8X4), scales=scales[:], in_=grouped[:])
+
+        def spread_bias():
+            for half in range(2):
+                cols = slice(512 * half, 512 * (half + 1))
+                spread = acc_pool.tile([P, 512], F32, name="spread", tag="acc")
+                nc.tensor.matmul(out=spread[:], lhsT=ones[:], rhs=bias_row[:, cols], start=True, stop=True)
+                nc.vector.tensor_copy(out=bias_all[:, cols], in_=spread[:])
+
+        def multiply(bank):
+            q, h = bank
+            acc = acc_pool.tile([P, 2, GROUP], F32, name="acc", tag="acc")
+            for j in range(2):
+                i = 2 * h + j
+                for g in range(PASSES):
+                    cols = slice(P * (g % 2), P * (g % 2 + 1))
                     nc.tensor.matmul_mx(
-                        out=dst,
-                        lhsT=xq[s][i][:, cols].bitcast(FP8X4),
-                        lhsT_scale=xs[s][i][:, cols],
-                        rhs=wq[q][g][:].bitcast(FP8X4),
-                        rhs_scale=ws[q][g][:],
+                        out=acc[:, j, :],
+                        lhsT=x_codes[g // 2][i][:, cols].bitcast(FP8X4),
+                        lhsT_scale=x_scales[g // 2][i][:, cols],
+                        rhs=w_codes[q][g][:].bitcast(FP8X4),
+                        rhs_scale=w_scales[q][g][:],
                         start=(g == 0),
-                        stop=(g == NG - 1),
+                        stop=(g == PASSES - 1),
                     )
-            elif kind == "E1":
-                q, ib, h = op[1], op[2], op[3]
-                bias = bias_bc[:, 256 * q : 256 * (q + 1)]
-                if h < 0:
-                    z = ep.tile([P, 2, 256], F32, name="z")
-                    nc.vector.tensor_tensor(
-                        out=z[:], in0=accs[(q, ib)][:], in1=bias.unsqueeze(1).to_broadcast([P, 2, 256]), op=ADD
-                    )
-                    zs[(q, ib, h)] = z
-                else:
-                    zh = ep.tile([P, 256], F32, name="zh")
-                    nc.vector.tensor_tensor(out=zh[:], in0=accs[(q, ib, h)][:], in1=bias, op=ADD)
-                    zs[(q, ib, h)] = zh
-            elif kind == "E2":
-                q, ib, h = op[1], op[2], op[3]
-                if h < 0:
-                    sg = ep.tile([P, 2, 256], F32, name="sg")
-                    nc.scalar.activation(out=sg[:], in_=zs[(q, ib, h)][:], func=SIGMOID)
-                    sgs[(q, ib, h)] = sg
-                else:
-                    sgh = ep.tile([P, 256], F32, name="sgh")
-                    nc.scalar.activation(out=sgh[:], in_=zs[(q, ib, h)][:], func=SIGMOID)
-                    sgs[(q, ib, h)] = sgh
-            elif kind == "E3":
-                q, ib, h = op[1], op[2], op[3]
-                eng = nc.gpsimd if op[4] == "G" else nc.vector
-                cols = slice(256 * q, 256 * (q + 1))
-                if h < 0:
-                    o = ep.tile([P, 2, 256], F32, name="o")
-                    eng.tensor_tensor(out=o[:], in0=sgs[(q, ib, h)][:], in1=x_sb[0][:, 2 * ib : 2 * ib + 2, cols], op=MULT)
-                    nc.sync.dma_start(out=ov[:, 2 * ib : 2 * ib + 2, cols], in_=o[:])
-                else:
-                    oh = ep.tile([P, 256], F32, name="oh")
-                    eng.tensor_tensor(out=oh[:], in0=sgs[(q, ib, h)][:], in1=x_sb[0][:, 2 * ib + h, cols], op=MULT)
-                    nc.sync.dma_start(out=ov[:, 2 * ib + h, cols], in_=oh[:])
+            return acc
+
+        def add_bias(bank, acc):
+            cols = slice(GROUP * bank[0], GROUP * (bank[0] + 1))
+            logits = gate_pool.tile([P, 2, GROUP], F32, name="logits")
+            nc.vector.tensor_tensor(
+                out=logits[:], in0=acc[:], in1=bias_all[:, cols].unsqueeze(1).to_broadcast([P, 2, GROUP]), op=ADD
+            )
+            return logits
+
+        def squash(logits):
+            gate = gate_pool.tile([P, 2, GROUP], F32, name="gate")
+            nc.scalar.activation(out=gate[:], in_=logits[:], func=SIGMOID)
+            return gate
+
+        def finish(bank, gate, engine):
+            q, h = bank
+            rows, cols = slice(2 * h, 2 * h + 2), slice(GROUP * q, GROUP * (q + 1))
+            result = gate_pool.tile([P, 2, GROUP], F32, name="result")
+            engine.tensor_tensor(out=result[:], in0=gate[:], in1=x_sb[0][:, rows, cols], op=MULT)
+            nc.sync.dma_start(out=out_dram[:, rows, cols], in_=result[:])
+
+        accs, logit_tiles, gates = {}, {}, {}
+        for r in range(-1, len(STAGES) + 2):
+            units = range(UNITS) if r + 1 < len(STAGES) else []
+            turned = [transpose_unit(r + 1, unit) for unit in units]
+            for bank in output_banks(r - 1):
+                logit_tiles[bank] = add_bias(bank, accs[bank])
+            last = output_banks(r - 2)
+            grouped = []
+            for unit in units:
+                grouped.append(copy_unit(r + 1, turned[unit]))
+                if unit > 0:
+                    quantise_unit(r + 1, unit - 1, grouped[unit - 1])
+            for bank in last:
+                finish(bank, gates[bank], nc.gpsimd if len(last) == 2 and bank == last[0] else nc.vector)
+            for bank in output_banks(r - 1):
+                gates[bank] = squash(logit_tiles[bank])
+            if grouped:
+                quantise_unit(r + 1, UNITS - 1, grouped[UNITS - 1])
+            if r == 0:
+                spread_bias()
+            for bank in output_banks(r):
+                accs[bank] = multiply(bank)

@@ -175,7 +175,8 @@ def tile_dynamicmemorycell_pa_kernel(tc, input_tensor, previous_memory, fg_w, fg
                 if unit > 0:
                     quantise_unit(r + 1, unit - 1, grouped[unit - 1])
             for bank in last:
-                finish(bank, gates[bank], nc.gpsimd if len(last) == 2 and bank == last[0] else nc.vector)
+                shared = len(last) == 2 and bank == last[0] and len(output_banks(r - 1)) > 0
+                finish(bank, gates[bank], nc.gpsimd if shared else nc.vector)
             for bank in output_banks(r - 1):
                 gates[bank] = squash(logit_tiles[bank])
             if grouped:

@@ -98,7 +98,7 @@ def tile_dynamicmemorycell_pa_kernel(tc, input_tensor, previous_memory, fg_w, fg
                 nc.tensor.transpose(turned[:, a, :], words[:, first : first + P], ident[:])
             return turned
 
-        def copy_unit(stage, turned):
+        def copy_unit(stage, unit, turned):
             grouped = grouped_pool.tile([P, 4 * 2 * P], BF16, name="grouped", align_bytes=64)
             if STAGES[stage][0] == "x":
                 dst = grouped[:].bitcast(F32).rearrange("p (g c u) -> p g c u", g=2, u=2)
@@ -106,7 +106,10 @@ def tile_dynamicmemorycell_pa_kernel(tc, input_tensor, previous_memory, fg_w, fg
             else:
                 dst = grouped[:].bitcast(F32).rearrange("p (c a) -> p c a", a=PER_BANK)
                 src = turned[:].rearrange("p a c -> p c a")
-            nc.scalar.copy(out=dst, in_=src)
+            if unit == 1:
+                nc.vector.tensor_copy(out=dst, in_=src)
+            else:
+                nc.scalar.copy(out=dst, in_=src)
             return grouped
 
         def quantise_unit(stage, unit, grouped):
@@ -171,7 +174,7 @@ def tile_dynamicmemorycell_pa_kernel(tc, input_tensor, previous_memory, fg_w, fg
             last = output_banks(r - 2)
             grouped = []
             for unit in units:
-                grouped.append(copy_unit(r + 1, turned[unit]))
+                grouped.append(copy_unit(r + 1, unit, turned[unit]))
                 if unit > 0:
                     quantise_unit(r + 1, unit - 1, grouped[unit - 1])
             for bank in last:

@@ -68,13 +68,12 @@ def tile_dynamicmemorycell_pa_kernel(tc, input_tensor, previous_memory, fg_w, fg
         w_sb = [keep.tile([P, 2, K], BF16, name="w_sb%d" % q) for q in range(GROUPS)]
         out_dram = out.rearrange("(p i) n -> p i n", i=ROW_TILES)
         for kind, index in STAGES:
-            for s in range(2):
-                if kind == "x":
-                    rows = slice(2 * index, 2 * index + 2)
+            if kind == "x":
+                rows = slice(2 * index, 2 * index + 2)
+                for s in range(2):
                     nc.sync.dma_start(out=x_sb[s][:, rows, :], in_=x_dram[s][:, rows, :])
-                else:
-                    cols = slice(MEM * s, MEM * (s + 1))
-                    nc.sync.dma_start(out=w_sb[index][:, :, cols], in_=w_dram[index][:, :, cols])
+            else:
+                nc.sync.dma_start(out=w_sb[index][:], in_=w_dram[index])
 
         def operand_tiles(label, dtype, outer, inner):
             return [
@@ -98,7 +97,7 @@ def tile_dynamicmemorycell_pa_kernel(tc, input_tensor, previous_memory, fg_w, fg
                 nc.tensor.transpose(turned[:, a, :], words[:, first : first + P], ident[:])
             return turned
 
-        def copy_unit(stage, unit, turned):
+        def copy_unit(stage, turned):
             grouped = grouped_pool.tile([P, 4 * 2 * P], BF16, name="grouped", align_bytes=64)
             if STAGES[stage][0] == "x":
                 dst = grouped[:].bitcast(F32).rearrange("p (g c u) -> p g c u", g=2, u=2)
@@ -106,10 +105,7 @@ def tile_dynamicmemorycell_pa_kernel(tc, input_tensor, previous_memory, fg_w, fg
             else:
                 dst = grouped[:].bitcast(F32).rearrange("p (c a) -> p c a", a=PER_BANK)
                 src = turned[:].rearrange("p a c -> p c a")
-            if unit == 1:
-                nc.vector.tensor_copy(out=dst, in_=src)
-            else:
-                nc.scalar.copy(out=dst, in_=src)
+            nc.scalar.copy(out=dst, in_=src)
             return grouped
 
         def quantise_unit(stage, unit, grouped):
@@ -174,7 +170,7 @@ def tile_dynamicmemorycell_pa_kernel(tc, input_tensor, previous_memory, fg_w, fg
             last = output_banks(r - 2)
             grouped = []
             for unit in units:
-                grouped.append(copy_unit(r + 1, unit, turned[unit]))
+                grouped.append(copy_unit(r + 1, turned[unit]))
                 if unit > 0:
                     quantise_unit(r + 1, unit - 1, grouped[unit - 1])
             for bank in last:

@@ -97,7 +97,7 @@ def tile_dynamicmemorycell_pa_kernel(tc, input_tensor, previous_memory, fg_w, fg
                 nc.tensor.transpose(turned[:, a, :], words[:, first : first + P], ident[:])
             return turned
 
-        def copy_unit(stage, turned):
+        def copy_unit(stage, unit, turned):
             grouped = grouped_pool.tile([P, 4 * 2 * P], BF16, name="grouped", align_bytes=64)
             if STAGES[stage][0] == "x":
                 dst = grouped[:].bitcast(F32).rearrange("p (g c u) -> p g c u", g=2, u=2)
@@ -105,7 +105,10 @@ def tile_dynamicmemorycell_pa_kernel(tc, input_tensor, previous_memory, fg_w, fg
             else:
                 dst = grouped[:].bitcast(F32).rearrange("p (c a) -> p c a", a=PER_BANK)
                 src = turned[:].rearrange("p a c -> p c a")
-            nc.scalar.copy(out=dst, in_=src)
+            if unit == 1:
+                nc.vector.tensor_copy(out=dst, in_=src)
+            else:
+                nc.scalar.copy(out=dst, in_=src)
             return grouped
 
         def quantise_unit(stage, unit, grouped):
@@ -170,7 +173,7 @@ def tile_dynamicmemorycell_pa_kernel(tc, input_tensor, previous_memory, fg_w, fg
             last = output_banks(r - 2)
             grouped = []
             for unit in units:
-                grouped.append(copy_unit(r + 1, turned[unit]))
+                grouped.append(copy_unit(r + 1, unit, turned[unit]))
                 if unit > 0:
                     quantise_unit(r + 1, unit - 1, grouped[unit - 1])
             for bank in last:

from contextlib import ExitStack

import concourse.mybir as mybir
from concourse.masks import make_identity

F32 = mybir.dt.float32
BF16 = mybir.dt.bfloat16
U32 = mybir.dt.uint32
U8 = mybir.dt.uint8
FP8X4 = mybir.dt.float8_e4m3fn_x4
ADD = mybir.AluOpType.add
MULT = mybir.AluOpType.mult
SIGMOID = mybir.ActivationFunctionType.Sigmoid

P = 128
B, IN, MEM = 512, 1024, 1024
K = MEM + IN
FLOPS = 2 * B * MEM * K

ROW_TILES = B // P
GROUP = 256
GROUPS = MEM // GROUP
PASSES = K // (4 * P)
WORDS = 2 * P
PER_BANK = 4
UNITS = 4

STAGES = (("x", 0), ("w", 0), ("x", 1), ("w", 1), ("w", 2), ("w", 3))


def output_banks(stage):
    if stage < 0 or stage >= len(STAGES):
        return []
    kind, index = STAGES[stage]
    seen = STAGES[:stage]
    if kind == "x":
        return [(q, index) for q in range(GROUPS) if ("w", q) in seen]
    return [(index, h) for h in range(2) if ("x", h) in seen]


def tile_dynamicmemorycell_pa_kernel(tc, input_tensor, previous_memory, fg_w, fg_b, out):
    nc = tc.nc
    with ExitStack() as ctx:
        const = ctx.enter_context(tc.tile_pool(name="const", bufs=1))
        keep = ctx.enter_context(tc.tile_pool(name="keep", bufs=1))
        grouped_pool = ctx.enter_context(tc.tile_pool(name="grouped_pool", bufs=6))
        gate_pool = ctx.enter_context(tc.tile_pool(name="gate_pool", bufs=4))
        turned_pool = ctx.enter_context(tc.psum_pool(name="turned_pool", bufs=5))
        acc_pool = ctx.enter_context(tc.psum_pool(name="acc_pool", bufs=3))
        ctx.enter_context(tc.manual_schedule())

        bias_row = const.tile([P, MEM], BF16, name="bias_row")
        nc.vector.memset(bias_row[:], 0.0)
        nc.scalar.dma_start(out=bias_row[0:1, :], in_=fg_b.unsqueeze(0))
        ones = const.tile([P, P], BF16, name="ones")
        nc.vector.memset(ones[:], 1.0)
        zero_col = const.tile([P, 1], F32, name="zero_col")
        nc.vector.memset(zero_col[:], 0.0)
        half_col = const.tile([P, 1], F32, name="half_col")
        nc.scalar.activation(out=half_col[:], in_=zero_col[:], func=SIGMOID)
        ident = const.tile([P, P], F32, name="ident")
        make_identity(nc, ident[:])
        bias_all = const.tile([P, MEM], F32, name="bias_all")

        x_dram = [a.rearrange("(p i) k -> p i k", i=ROW_TILES) for a in (previous_memory, input_tensor)]
        x_sb = [keep.tile([P, ROW_TILES, MEM], BF16, name="x_sb%d" % s) for s in range(2)]
        w_dram = fg_w.rearrange("(q c r) k -> q c r k", q=GROUPS, r=2)
        w_sb = [keep.tile([P, 2, K], BF16, name="w_sb%d" % q) for q in range(GROUPS)]
        out_dram = out.rearrange("(p i) n -> p i n", i=ROW_TILES)
        for kind, index in STAGES:
            if kind == "x":
                rows = slice(2 * index, 2 * index + 2)
                for s in range(2):
                    nc.sync.dma_start(out=x_sb[s][:, rows, :], in_=x_dram[s][:, rows, :])
            else:
                nc.sync.dma_start(out=w_sb[index][:], in_=w_dram[index])

        def operand_tiles(label, dtype, outer, inner):
            return [
                [keep.tile([P, GROUP], dtype, name="%s%d_%d" % (label, a, b), align_bytes=64) for b in range(inner)]
                for a in range(outer)
            ]

        x_codes, x_scales = operand_tiles("x_codes", U32, 2, ROW_TILES), operand_tiles("x_scales", U8, 2, ROW_TILES)
        w_codes, w_scales = operand_tiles("w_codes", U32, GROUPS, PASSES), operand_tiles("w_scales", U8, GROUPS, PASSES)

        def transpose_unit(stage, unit):
            kind, index = STAGES[stage]
            turned = turned_pool.tile([P, PER_BANK, P], F32, name="turned")
            for a in range(PER_BANK):
                if kind == "x":
                    words = x_sb[unit // 2][:, 2 * index + unit % 2, :].bitcast(F32)
                    first = P * a
                else:
                    words = w_sb[index][:, a // 2, :].bitcast(F32)
                    first = WORDS * unit + P * (a % 2)
                nc.tensor.transpose(turned[:, a, :], words[:, first : first + P], ident[:])
            return turned

        def copy_unit(stage, unit, turned):
            grouped = grouped_pool.tile([P, 4 * 2 * P], BF16, name="grouped", align_bytes=64)
            if STAGES[stage][0] == "x":
                dst = grouped[:].bitcast(F32).rearrange("p (g c u) -> p g c u", g=2, u=2)
                src = turned[:].rearrange("p (g u) c -> p g c u", g=2)
            else:
                dst = grouped[:].bitcast(F32).rearrange("p (c a) -> p c a", a=PER_BANK)
                src = turned[:].rearrange("p a c -> p c a")
            if unit == 1:
                nc.vector.tensor_copy(out=dst, in_=src)
            else:
                nc.scalar.copy(out=dst, in_=src)
            return grouped

        def quantise_unit(stage, unit, grouped):
            kind, index = STAGES[stage]
            if kind == "x":
                codes, scales = x_codes[unit // 2][2 * index + unit % 2], x_scales[unit // 2][2 * index + unit % 2]
            else:
                codes, scales = w_codes[index][unit], w_scales[index][unit]
            nc.vector.quantize_mx(out=codes[:].bitcast(FP8X4), scales=scales[:], in_=grouped[:])

        def spread_bias():
            for half in range(2):
                cols = slice(512 * half, 512 * (half + 1))
                spread = acc_pool.tile([P, 512], F32, name="spread", tag="acc")
                nc.tensor.matmul(out=spread[:], lhsT=ones[:], rhs=bias_row[:, cols], start=True, stop=True)
                nc.vector.tensor_copy(out=bias_all[:, cols], in_=spread[:])

        def multiply(bank):
            q, h = bank
            acc = acc_pool.tile([P, 2, GROUP], F32, name="acc", tag="acc")
            for j in range(2):
                i = 2 * h + j
                for g in range(PASSES):
                    cols = slice(P * (g % 2), P * (g % 2 + 1))
                    nc.tensor.matmul_mx(
                        out=acc[:, j, :],
                        lhsT=x_codes[g // 2][i][:, cols].bitcast(FP8X4),
                        lhsT_scale=x_scales[g // 2][i][:, cols],
                        rhs=w_codes[q][g][:].bitcast(FP8X4),
                        rhs_scale=w_scales[q][g][:],
                        start=(g == 0),
                        stop=(g == PASSES - 1),
                    )
            return acc

        def add_bias(bank, acc):
            cols = slice(GROUP * bank[0], GROUP * (bank[0] + 1))
            logits = gate_pool.tile([P, 2, GROUP], F32, name="logits")
            nc.vector.tensor_tensor(
                out=logits[:], in0=acc[:], in1=bias_all[:, cols].unsqueeze(1).to_broadcast([P, 2, GROUP]), op=ADD
            )
            return logits

        def squash(logits):
            gate = gate_pool.tile([P, 2, GROUP], F32, name="gate")
            nc.scalar.activation(out=gate[:], in_=logits[:], func=SIGMOID)
            return gate

        def finish(bank, gate, engine):
            q, h = bank
            rows, cols = slice(2 * h, 2 * h + 2), slice(GROUP * q, GROUP * (q + 1))
            result = gate_pool.tile([P, 2, GROUP], F32, name="result")
            engine.tensor_tensor(out=result[:], in0=gate[:], in1=x_sb[0][:, rows, cols], op=MULT)
            nc.sync.dma_start(out=out_dram[:, rows, cols], in_=result[:])

        accs, logit_tiles, gates = {}, {}, {}
        for r in range(-1, len(STAGES) + 2):
            units = range(UNITS) if r + 1 < len(STAGES) else []
            turned = [transpose_unit(r + 1, unit) for unit in units]
            for bank in output_banks(r - 1):
                logit_tiles[bank] = add_bias(bank, accs[bank])
            last = output_banks(r - 2)
            grouped = []
            for unit in units:
                grouped.append(copy_unit(r + 1, unit, turned[unit]))
                if unit > 0:
                    quantise_unit(r + 1, unit - 1, grouped[unit - 1])
            for bank in last:
                shared = len(last) == 2 and bank == last[0] and len(output_banks(r - 1)) > 0
                finish(bank, gates[bank], nc.gpsimd if shared else nc.vector)
            for bank in output_banks(r - 1):
                gates[bank] = squash(logit_tiles[bank])
            if grouped:
                quantise_unit(r + 1, UNITS - 1, grouped[UNITS - 1])
            if r == 0:
                spread_bias()
            for bank in output_banks(r):
                accs[bank] = multiply(bank)
